import numpy as np
import ml_dtypes


def mxq(x, axis, fmt="e4m3"):
    dtype, down = {"e4m3": (ml_dtypes.float8_e4m3fn, 7), "e5m2": (ml_dtypes.float8_e5m2, 14)}[fmt]
    v = np.moveaxis(np.asarray(x, np.float32).astype(ml_dtypes.bfloat16).astype(np.float64), axis, -1)
    blocks = v.reshape(v.shape[:-1] + (-1, 32))
    amax = np.abs(blocks).max(-1, keepdims=True)
    byte = np.maximum(np.where(amax > 0, np.frexp(amax)[1] - 1 + 127, 0) - down, 1)
    scale = np.exp2(byte - 127.0)
    codes = (blocks / scale).astype(np.float32).astype(dtype).astype(np.float64)
    return np.moveaxis((codes * scale).reshape(v.shape), -1, axis)


WIDE = False


def mx_kscale(k):
    if not WIDE:
        return np.ones(k)
    levels = np.array([10, -10, 5, -5, 0])
    a = np.random.permutation(np.resize(levels, k // 512 * 4)).reshape(k // 512, 4)
    idx = np.arange(k)
    return np.exp2(a[idx // 512, idx % 128 // 32])


BF16 = ml_dtypes.bfloat16


def bf(x):
    return np.asarray(x, np.float32).astype(BF16)


def f64(x):
    return np.asarray(x).astype(np.float64)


B, N, C, H = 2, 128, 2048, 16
EPS = 1e-6


def rmsnorm(v, w):
    var = np.mean(np.square(v), axis=-1, keepdims=True)
    return v * (1.0 / np.sqrt(var + EPS)) * w


def setup_inputs():
    s = mx_kscale(C)
    return {"x": bf(np.random.standard_normal((B, N, C)) * s),
            "w_qkv": bf(np.random.standard_normal((3 * C, C)) / np.sqrt(C) / s[None, :]),
            "q_norm_w": bf(1.0 + 0.1 * np.random.standard_normal(C)),
            "k_norm_w": bf(1.0 + 0.1 * np.random.standard_normal(C))}


def reference(x, w_qkv, q_norm_w, k_norm_w):
    xq = mxq(f64(x), 2, "e4m3")
    wt = f64(w_qkv).T
    q = xq @ mxq(wt[:, :C], 0, "e4m3")
    k = xq @ mxq(wt[:, C:2 * C], 0, "e4m3")
    v = xq @ mxq(wt[:, 2 * C:], 0, "e4m3")
    return rmsnorm(q, f64(q_norm_w)), rmsnorm(k, f64(k_norm_w)), v

@@ -1,0 +1,221 @@
+from contextlib import ExitStack
+
+import concourse.mybir as mybir
+from concourse.masks import make_identity
+
+F32 = mybir.dt.float32
+BF16 = mybir.dt.bfloat16
+U32 = mybir.dt.uint32
+U8 = mybir.dt.uint8
+FP8X4 = mybir.dt.float8_e4m3fn_x4
+ALU = mybir.AluOpType
+ACT = mybir.ActivationFunctionType
+
+P = 128
+HIDDEN = 2048
+TOKENS = 256
+EPS = 1e-6
+PACK = 4
+K_PASS = P * PACK
+PASSES = HIDDEN // K_PASS
+WORDS_PER_PASS = K_PASS // 2
+ROWS_PER_PARTITION = 2
+UNIT = P * ROWS_PER_PARTITION
+TOKEN_TILES = TOKENS // P
+CHUNK = 512
+UNITS_PER_CHUNK = CHUNK // UNIT
+CHUNKS_PER_PART = HIDDEN // CHUNK
+PARTS = 3
+NORMED_PARTS = 2
+CHUNKS = PARTS * CHUNKS_PER_PART
+CHUNKS_AHEAD = 3
+VECTOR_PASS = PASSES - 1
+
+FLOPS = 2 * TOKENS * HIDDEN * PARTS * HIDDEN
+
+
+def as_multiplied(columns):
+    return columns.rearrange("m (h j p) -> m h p j", h=UNITS_PER_CHUNK, j=ROWS_PER_PARTITION)
+
+
+def as_stored(columns):
+    return columns.rearrange("m (h p j) -> m h p j", h=UNITS_PER_CHUNK, j=ROWS_PER_PARTITION)
+
+
+def tile_internattention_pa_kernel(tc, x, w_qkv, q_norm_w, k_norm_w, out_0, out_1, out_2):
+    nc = tc.nc
+    x_rows = x.flatten_outer_dims()
+    outs = [
+        out.flatten_outer_dims().rearrange("(p t) n -> p t n", t=TOKEN_TILES)
+        for out in (out_0, out_1, out_2)
+    ]
+    gain_rows = [q_norm_w, k_norm_w]
+
+    with ExitStack() as ctx:
+        const = ctx.enter_context(tc.tile_pool(name="const", bufs=1))
+        raw_pool = ctx.enter_context(tc.tile_pool(name="raw", bufs=UNITS_PER_CHUNK * (CHUNKS_AHEAD + 1)))
+        grouped_pool = ctx.enter_context(tc.tile_pool(name="grouped", bufs=4))
+        codes_pool = ctx.enter_context(tc.tile_pool(name="codes", bufs=3))
+        normed_pool = ctx.enter_context(tc.tile_pool(name="normed", bufs=NORMED_PARTS * TOKEN_TILES))
+        plain_pool = ctx.enter_context(tc.tile_pool(name="plain", bufs=4))
+        squares_pool = ctx.enter_context(tc.tile_pool(name="squares", bufs=4))
+        stats_pool = ctx.enter_context(tc.tile_pool(name="stats", bufs=NORMED_PARTS))
+        bank_pool = ctx.enter_context(tc.psum_pool(name="bank", bufs=6))
+        acc_pool = ctx.enter_context(tc.psum_pool(name="acc", bufs=TOKEN_TILES))
+
+        identity = const.tile([P, P], F32)
+        make_identity(nc, identity[:])
+        ones = const.tile([P, 1], F32)
+        nc.vector.memset(ones[:], 1.0)
+        warm = const.tile([P, 1], F32)
+        nc.scalar.sqrt(out=warm[:], in_=ones[:])
+
+        x_codes = const.tile([P, PASSES, UNIT], U32, align_bytes=64)
+        x_scales = const.tile([P, PASSES, UNIT], U8, align_bytes=64)
+        gains = [const.tile([P, HIDDEN], BF16, name="gain%d" % part) for part in range(NORMED_PARTS)]
+
+        def load_unit(rows):
+            raw = raw_pool.tile([P, ROWS_PER_PARTITION, HIDDEN], BF16)
+            nc.sync.dma_start(out=raw[:], in_=rows.rearrange("(p j) k -> p j k", j=ROWS_PER_PARTITION))
+            return raw
+
+        def load_chunk(c):
+            first = c * CHUNK
+            raws = [load_unit(w_qkv[first + h * UNIT : first + (h + 1) * UNIT, :]) for h in range(UNITS_PER_CHUNK)]
+            part = c // CHUNKS_PER_PART
+            if part < NORMED_PARTS and c % CHUNKS_PER_PART == 1:
+                nc.sync.dma_start(out=gains[part][:], in_=gain_rows[part].partition_broadcast(P))
+            return raws
+
+        def regroup_unit(raw):
+            grouped = grouped_pool.tile([P, PASSES, UNIT * PACK], BF16, align_bytes=64)
+            for g in range(PASSES):
+                bank = bank_pool.tile([P, 2, UNIT], F32)
+                for u in range(2):
+                    first_word = g * WORDS_PER_PASS + u * P
+                    for j in range(ROWS_PER_PARTITION):
+                        nc.tensor.transpose(
+                            bank[:, u, j * P : (j + 1) * P],
+                            raw[:, j, :].bitcast(F32)[:, first_word : first_word + P],
+                            identity[:],
+                        )
+                pairs = grouped[:, g, :].bitcast(F32).rearrange("p (r u) -> p r u", u=2)
+                if g == VECTOR_PASS:
+                    nc.vector.tensor_copy(out=pairs, in_=bank[:].rearrange("p u r -> p r u"))
+                else:
+                    nc.scalar.copy(out=pairs, in_=bank[:].rearrange("p u r -> p r u"))
+            return grouped
+
+        def quantise_unit(grouped, codes, scales, h):
+            columns = slice(h * UNIT, (h + 1) * UNIT)
+            for g in range(PASSES):
+                nc.vector.quantize_mx(
+                    out=codes[:, g, columns].bitcast(FP8X4),
+                    scales=scales[:, g, columns],
+                    in_=grouped[:, g, :],
+                )
+
+        def multiply(codes, scales):
+            accs = []
+            for t in range(TOKEN_TILES):
+                acc = acc_pool.tile([P, CHUNK], F32)
+                for g in range(PASSES):
+                    nc.tensor.matmul_mx(
+                        out=acc[:],
+                        lhsT=x_codes[:, g, t * P : (t + 1) * P].bitcast(FP8X4),
+                        lhsT_scale=x_scales[:, g, t * P : (t + 1) * P],
+                        rhs=codes[:, g, :].bitcast(FP8X4),
+                        rhs_scale=scales[:, g, :],
+                        start=(g == 0),
+                        stop=(g == PASSES - 1),
+                    )
+                accs.append(acc)
+            return accs
+
+        def take_normed(accs, part, i, sumsq, normed):
+            columns = slice(i * CHUNK, (i + 1) * CHUNK)
+            for t in range(TOKEN_TILES):
+                squares = squares_pool.tile([P, CHUNK], BF16)
+                nc.scalar.activation(
+                    out=squares[:], in_=accs[t][:], func=ACT.Square, accum_out=sumsq[:, t, i : i + 1]
+                )
+                nc.vector.tensor_tensor(
+                    out=as_stored(normed[t][:, columns]),
+                    in0=as_multiplied(accs[t][:]),
+                    in1=as_stored(gains[part][:, columns]),
+                    op=ALU.mult,
+                )
+
+        def take_plain(accs, i):
+            columns = slice(i * CHUNK, (i + 1) * CHUNK)
+            for t in range(TOKEN_TILES):
+                plain = plain_pool.tile([P, CHUNK], F32)
+                if t == 0:
+                    nc.scalar.copy(out=as_stored(plain[:]), in_=as_multiplied(accs[t][:]))
+                else:
+                    nc.vector.tensor_copy(out=as_stored(plain[:]), in_=as_multiplied(accs[t][:]))
+                nc.sync.dma_start(out=outs[PARTS - 1][:, t, columns], in_=plain[:])
+
+        def root_mean_square(sumsq):
+            total = stats_pool.tile([P, TOKEN_TILES], F32)
+            nc.vector.tensor_reduce(out=total[:], in_=sumsq[:], axis=mybir.AxisListType.X, op=ALU.add)
+            mean = stats_pool.tile([P, TOKEN_TILES], F32)
+            nc.vector.tensor_scalar(
+                out=mean[:], in0=total[:], scalar1=1.0 / HIDDEN, scalar2=EPS, op0=ALU.mult, op1=ALU.add
+            )
+            rms = stats_pool.tile([P, TOKEN_TILES], F32)
+            nc.scalar.sqrt(out=rms[:], in_=mean[:])
+            return rms
+
+        def divide_and_store(part, rms, normed):
+            inverse = stats_pool.tile([P, TOKEN_TILES], F32)
+            nc.vector.reciprocal(out=inverse[:], in_=rms[:])
+            for t in range(TOKEN_TILES):
+                nc.vector.tensor_scalar_mul(out=normed[t][:], in0=normed[t][:], scalar1=inverse[:, t : t + 1])
+                nc.sync.dma_start(out=outs[part][:, t, :], in_=normed[t][:])
+
+        ctx.enter_context(tc.manual_schedule())
+
+        x_raw = load_unit(x_rows)
+        raws = {}
+        for c in range(CHUNKS_AHEAD):
+            raws[c] = load_chunk(c)
+
+        not_quantised = (regroup_unit(x_raw), x_codes, x_scales, 0)
+        operands = {}
+        sumsq = None
+        normed = None
+        waiting = None
+        for c in range(CHUNKS + 1):
+            if c + CHUNKS_AHEAD < CHUNKS:
+                raws[c + CHUNKS_AHEAD] = load_chunk(c + CHUNKS_AHEAD)
+
+            if c < CHUNKS:
+                codes = codes_pool.tile([P, PASSES, CHUNK], U32, align_bytes=64)
+                scales = codes_pool.tile([P, PASSES, CHUNK], U8, align_bytes=64)
+                operands[c] = (codes, scales)
+                for h in range(UNITS_PER_CHUNK):
+                    grouped = regroup_unit(raws[c][h])
+                    quantise_unit(*not_quantised)
+                    not_quantised = (grouped, codes, scales, h)
+            else:
+                quantise_unit(*not_quantised)
+
+            if c == 0:
+                continue
+            done = c - 1
+            part = done // CHUNKS_PER_PART
+            i = done % CHUNKS_PER_PART
+            accs = multiply(*operands[done])
+            if part == NORMED_PARTS:
+                take_plain(accs, i)
+            else:
+                if i == 0:
+                    sumsq = stats_pool.tile([P, TOKEN_TILES, CHUNKS_PER_PART], F32)
+                    normed = [normed_pool.tile([P, HIDDEN], F32, name="normed") for t in range(TOKEN_TILES)]
+                take_normed(accs, part, i, sumsq, normed)
+            if waiting is not None:
+                divide_and_store(*waiting)
+                waiting = None
+            if part < NORMED_PARTS and i == CHUNKS_PER_PART - 1:
+                waiting = (part, root_mean_square(sumsq), normed)

@@ -115,46 +115,36 @@ def tile_internattention_pa_kernel(tc, x, w_qkv, q_norm_w, k_norm_w, out_0, out_
                     in_=grouped[:, g, :],
                 )
 
-        def multiply(codes, scales):
-            accs = []
-            for t in range(TOKEN_TILES):
-                acc = acc_pool.tile([P, CHUNK], F32)
-                for g in range(PASSES):
-                    nc.tensor.matmul_mx(
-                        out=acc[:],
-                        lhsT=x_codes[:, g, t * P : (t + 1) * P].bitcast(FP8X4),
-                        lhsT_scale=x_scales[:, g, t * P : (t + 1) * P],
-                        rhs=codes[:, g, :].bitcast(FP8X4),
-                        rhs_scale=scales[:, g, :],
-                        start=(g == 0),
-                        stop=(g == PASSES - 1),
-                    )
-                accs.append(acc)
-            return accs
-
-        def take_normed(accs, part, i, sumsq, normed):
-            columns = slice(i * CHUNK, (i + 1) * CHUNK)
-            for t in range(TOKEN_TILES):
-                squares = squares_pool.tile([P, CHUNK], BF16)
-                nc.scalar.activation(
-                    out=squares[:], in_=accs[t][:], func=ACT.Square, accum_out=sumsq[:, t, i : i + 1]
+        def multiply(t, codes, scales):
+            acc = acc_pool.tile([P, CHUNK], F32)
+            for g in range(PASSES):
+                nc.tensor.matmul_mx(
+                    out=acc[:],
+                    lhsT=x_codes[:, g, t * P : (t + 1) * P].bitcast(FP8X4),
+                    lhsT_scale=x_scales[:, g, t * P : (t + 1) * P],
+                    rhs=codes[:, g, :].bitcast(FP8X4),
+                    rhs_scale=scales[:, g, :],
+                    start=(g == 0),
+                    stop=(g == PASSES - 1),
                 )
-                nc.vector.tensor_tensor(
-                    out=as_stored(normed[t][:, columns]),
-                    in0=as_multiplied(accs[t][:]),
-                    in1=as_stored(gains[part][:, columns]),
-                    op=ALU.mult,
-                )
+            return acc
 
-        def take_plain(accs, i):
+        def take_normed(acc, t, part, i, sumsq, normed):
             columns = slice(i * CHUNK, (i + 1) * CHUNK)
-            for t in range(TOKEN_TILES):
-                plain = plain_pool.tile([P, CHUNK], F32)
-                if t == 0:
-                    nc.scalar.copy(out=as_stored(plain[:]), in_=as_multiplied(accs[t][:]))
-                else:
-                    nc.vector.tensor_copy(out=as_stored(plain[:]), in_=as_multiplied(accs[t][:]))
-                nc.sync.dma_start(out=outs[PARTS - 1][:, t, columns], in_=plain[:])
+            squares = squares_pool.tile([P, CHUNK], BF16)
+            nc.scalar.activation(out=squares[:], in_=acc[:], func=ACT.Square, accum_out=sumsq[:, t, i : i + 1])
+            nc.vector.tensor_tensor(
+                out=as_stored(normed[t][:, columns]),
+                in0=as_multiplied(acc[:]),
+                in1=as_stored(gains[part][:, columns]),
+                op=ALU.mult,
+            )
+
+        def take_plain(acc, t, i):
+            columns = slice(i * CHUNK, (i + 1) * CHUNK)
+            plain = plain_pool.tile([P, CHUNK], F32)
+            nc.scalar.copy(out=as_stored(plain[:]), in_=as_multiplied(acc[:]))
+            nc.sync.dma_start(out=outs[PARTS - 1][:, t, columns], in_=plain[:])
 
         def root_mean_square(sumsq):
             total = stats_pool.tile([P, TOKEN_TILES], F32)
@@ -167,12 +157,11 @@ def tile_internattention_pa_kernel(tc, x, w_qkv, q_norm_w, k_norm_w, out_0, out_
             nc.scalar.sqrt(out=rms[:], in_=mean[:])
             return rms
 
-        def divide_and_store(part, rms, normed):
-            inverse = stats_pool.tile([P, TOKEN_TILES], F32)
-            nc.vector.reciprocal(out=inverse[:], in_=rms[:])
-            for t in range(TOKEN_TILES):
-                nc.vector.tensor_scalar_mul(out=normed[t][:], in0=normed[t][:], scalar1=inverse[:, t : t + 1])
-                nc.sync.dma_start(out=outs[part][:, t, :], in_=normed[t][:])
+        def divide_and_store(t, part, rms, normed):
+            inverse = stats_pool.tile([P, 1], F32)
+            nc.vector.reciprocal(out=inverse[:], in_=rms[:, t : t + 1])
+            nc.vector.tensor_scalar_mul(out=normed[t][:], in0=normed[t][:], scalar1=inverse[:])
+            nc.sync.dma_start(out=outs[part][:, t, :], in_=normed[t][:])
 
         ctx.enter_context(tc.manual_schedule())
 
@@ -181,41 +170,39 @@ def tile_internattention_pa_kernel(tc, x, w_qkv, q_norm_w, k_norm_w, out_0, out_
         for c in range(CHUNKS_AHEAD):
             raws[c] = load_chunk(c)
 
-        not_quantised = (regroup_unit(x_raw), x_codes, x_scales, 0)
+        quantise_unit(regroup_unit(x_raw), x_codes, x_scales, 0)
+
         operands = {}
         sumsq = None
         normed = None
-        waiting = None
+        undivided = None
         for c in range(CHUNKS + 1):
             if c + CHUNKS_AHEAD < CHUNKS:
                 raws[c + CHUNKS_AHEAD] = load_chunk(c + CHUNKS_AHEAD)
-
             if c < CHUNKS:
                 codes = codes_pool.tile([P, PASSES, CHUNK], U32, align_bytes=64)
                 scales = codes_pool.tile([P, PASSES, CHUNK], U8, align_bytes=64)
                 operands[c] = (codes, scales)
-                for h in range(UNITS_PER_CHUNK):
-                    grouped = regroup_unit(raws[c][h])
-                    quantise_unit(*not_quantised)
-                    not_quantised = (grouped, codes, scales, h)
-            else:
-                quantise_unit(*not_quantised)
+            part = (c - 1) // CHUNKS_PER_PART
+            i = (c - 1) % CHUNKS_PER_PART
+            if c > 0 and part < NORMED_PARTS and i == 0:
+                sumsq = stats_pool.tile([P, TOKEN_TILES, CHUNKS_PER_PART], F32)
+                normed = [normed_pool.tile([P, HIDDEN], F32, name="normed") for t in range(TOKEN_TILES)]
 
-            if c == 0:
-                continue
-            done = c - 1
-            part = done // CHUNKS_PER_PART
-            i = done % CHUNKS_PER_PART
-            accs = multiply(*operands[done])
-            if part == NORMED_PARTS:
-                take_plain(accs, i)
-            else:
-                if i == 0:
-                    sumsq = stats_pool.tile([P, TOKEN_TILES, CHUNKS_PER_PART], F32)
-                    normed = [normed_pool.tile([P, HIDDEN], F32, name="normed") for t in range(TOKEN_TILES)]
-                take_normed(accs, part, i, sumsq, normed)
-            if waiting is not None:
-                divide_and_store(*waiting)
-                waiting = None
-            if part < NORMED_PARTS and i == CHUNKS_PER_PART - 1:
-                waiting = (part, root_mean_square(sumsq), normed)
+            for h in range(UNITS_PER_CHUNK):
+                if c < CHUNKS:
+                    grouped = regroup_unit(raws[c][h])
+                if c > 0:
+                    acc = multiply(h, *operands[c - 1])
+                if c < CHUNKS:
+                    quantise_unit(grouped, codes, scales, h)
+                if c > 0 and part < NORMED_PARTS:
+                    take_normed(acc, h, part, i, sumsq, normed)
+                if c > 0 and part == NORMED_PARTS:
+                    take_plain(acc, h, i)
+                if undivided is not None:
+                    divide_and_store(h, *undivided)
+
+            undivided = None
+            if c > 0 and part < NORMED_PARTS and i == CHUNKS_PER_PART - 1:
+                undivided = (part, root_mean_square(sumsq), normed)

@@ -28,8 +28,11 @@ CHUNKS_PER_PART = HIDDEN // CHUNK
 PARTS = 3
 NORMED_PARTS = 2
 CHUNKS = PARTS * CHUNKS_PER_PART
+UNITS = CHUNKS * UNITS_PER_CHUNK
 CHUNKS_AHEAD = 3
-VECTOR_PASS = PASSES - 1
+QUANTISE_LAG = 1
+MULTIPLY_LAG = 3
+TAKE_LAG = 4
 
 FLOPS = 2 * TOKENS * HIDDEN * PARTS * HIDDEN
 
@@ -87,7 +90,7 @@ def tile_internattention_pa_kernel(tc, x, w_qkv, q_norm_w, k_norm_w, out_0, out_
                 nc.sync.dma_start(out=gains[part][:], in_=gain_rows[part].partition_broadcast(P))
             return raws
 
-        def regroup_unit(raw):
+        def regroup_unit(raw, vector_helps):
             grouped = grouped_pool.tile([P, PASSES, UNIT * PACK], BF16, align_bytes=64)
             for g in range(PASSES):
                 bank = bank_pool.tile([P, 2, UNIT], F32)
@@ -100,7 +103,7 @@ def tile_internattention_pa_kernel(tc, x, w_qkv, q_norm_w, k_norm_w, out_0, out_
                             identity[:],
                         )
                 pairs = grouped[:, g, :].bitcast(F32).rearrange("p (r u) -> p r u", u=2)
-                if g == VECTOR_PASS:
+                if vector_helps and g == PASSES - 1:
                     nc.vector.tensor_copy(out=pairs, in_=bank[:].rearrange("p u r -> p r u"))
                 else:
                     nc.scalar.copy(out=pairs, in_=bank[:].rearrange("p u r -> p r u"))
@@ -166,43 +169,57 @@ def tile_internattention_pa_kernel(tc, x, w_qkv, q_norm_w, k_norm_w, out_0, out_
         ctx.enter_context(tc.manual_schedule())
 
         x_raw = load_unit(x_rows)
-        raws = {}
+        raws = []
         for c in range(CHUNKS_AHEAD):
-            raws[c] = load_chunk(c)
+            raws.extend(load_chunk(c))
 
-        quantise_unit(regroup_unit(x_raw), x_codes, x_scales, 0)
+        quantise_unit(regroup_unit(x_raw, True), x_codes, x_scales, 0)
 
+        regrouped = {}
         operands = {}
-        sumsq = None
-        normed = None
-        undivided = None
-        for c in range(CHUNKS + 1):
-            if c + CHUNKS_AHEAD < CHUNKS:
-                raws[c + CHUNKS_AHEAD] = load_chunk(c + CHUNKS_AHEAD)
-            if c < CHUNKS:
-                codes = codes_pool.tile([P, PASSES, CHUNK], U32, align_bytes=64)
-                scales = codes_pool.tile([P, PASSES, CHUNK], U8, align_bytes=64)
-                operands[c] = (codes, scales)
-            part = (c - 1) // CHUNKS_PER_PART
-            i = (c - 1) % CHUNKS_PER_PART
-            if c > 0 and part < NORMED_PARTS and i == 0:
-                sumsq = stats_pool.tile([P, TOKEN_TILES, CHUNKS_PER_PART], F32)
-                normed = [normed_pool.tile([P, HIDDEN], F32, name="normed") for t in range(TOKEN_TILES)]
+        accs = {}
+        sumsq = {}
+        normed = {}
+        rms = {}
+        for s in range(UNITS + TAKE_LAG):
+            if s % UNITS_PER_CHUNK == 0 and s // UNITS_PER_CHUNK + CHUNKS_AHEAD < CHUNKS:
+                raws.extend(load_chunk(s // UNITS_PER_CHUNK + CHUNKS_AHEAD))
 
-            for h in range(UNITS_PER_CHUNK):
-                if c < CHUNKS:
-                    grouped = regroup_unit(raws[c][h])
-                if c > 0:
-                    acc = multiply(h, *operands[c - 1])
-                if c < CHUNKS:
-                    quantise_unit(grouped, codes, scales, h)
-                if c > 0 and part < NORMED_PARTS:
-                    take_normed(acc, h, part, i, sumsq, normed)
-                if c > 0 and part == NORMED_PARTS:
-                    take_plain(acc, h, i)
-                if undivided is not None:
-                    divide_and_store(h, *undivided)
+            unit = s - QUANTISE_LAG
+            if 0 <= unit < UNITS:
+                c = unit // UNITS_PER_CHUNK
+                if unit % UNITS_PER_CHUNK == 0:
+                    codes = codes_pool.tile([P, PASSES, CHUNK], U32, align_bytes=64)
+                    scales = codes_pool.tile([P, PASSES, CHUNK], U8, align_bytes=64)
+                    operands[c] = (codes, scales)
+                quantise_unit(regrouped[unit], *operands[c], unit % UNITS_PER_CHUNK)
 
-            undivided = None
-            if c > 0 and part < NORMED_PARTS and i == CHUNKS_PER_PART - 1:
-                undivided = (part, root_mean_square(sumsq), normed)
+            job = s - TAKE_LAG
+            if 0 <= job < UNITS:
+                t = job % TOKEN_TILES
+                part = job // TOKEN_TILES // CHUNKS_PER_PART
+                i = job // TOKEN_TILES % CHUNKS_PER_PART
+                if part < NORMED_PARTS:
+                    if i == 0 and t == 0:
+                        sumsq[part] = stats_pool.tile([P, TOKEN_TILES, CHUNKS_PER_PART], F32, name="sumsq")
+                        normed[part] = [
+                            normed_pool.tile([P, HIDDEN], F32, name="normed") for each in range(TOKEN_TILES)
+                        ]
+                    take_normed(accs[job], t, part, i, sumsq[part], normed[part])
+                else:
+                    take_plain(accs[job], t, i)
+                if i == 0 and part > 0:
+                    divide_and_store(t, part - 1, rms[part - 1], normed[part - 1])
+
+            if s < UNITS:
+                regrouped[s] = regroup_unit(raws[s], s % 2 == 1)
+
+            job = s - MULTIPLY_LAG
+            if 0 <= job < UNITS:
+                accs[job] = multiply(job % TOKEN_TILES, *operands[job // TOKEN_TILES])
+
+            job = s - TAKE_LAG
+            if job >= 0 and job % (TOKEN_TILES * CHUNKS_PER_PART) == TOKEN_TILES * CHUNKS_PER_PART - 1:
+                part = job // TOKEN_TILES // CHUNKS_PER_PART
+                if part < NORMED_PARTS:
+                    rms[part] = root_mean_square(sumsq[part])

@@ -52,7 +52,7 @@ def tile_internattention_pa_kernel(tc, x, w_qkv, q_norm_w, k_norm_w, out_0, out_
         out.flatten_outer_dims().rearrange("(p t) n -> p t n", t=TOKEN_TILES)
         for out in (out_0, out_1, out_2)
     ]
-    gain_rows = [q_norm_w, k_norm_w]
+    gain_vectors = [q_norm_w, k_norm_w]
 
     with ExitStack() as ctx:
         const = ctx.enter_context(tc.tile_pool(name="const", bufs=1))
@@ -68,14 +68,32 @@ def tile_internattention_pa_kernel(tc, x, w_qkv, q_norm_w, k_norm_w, out_0, out_
 
         identity = const.tile([P, P], F32)
         make_identity(nc, identity[:])
+        x_codes = const.tile([P, PASSES, UNIT], U32, align_bytes=64)
+        x_scales = const.tile([P, PASSES, UNIT], U8, align_bytes=64)
+
+        gain_rows = [const.tile([P, HIDDEN], BF16, name="gain_row%d" % part) for part in range(NORMED_PARTS)]
+        gains = [const.tile([P, HIDDEN], BF16, name="gain%d" % part) for part in range(NORMED_PARTS)]
+        for part in range(NORMED_PARTS):
+            nc.vector.memset(gain_rows[part][:], 0.0)
+            nc.scalar.dma_start(out=gain_rows[part][0:1, :], in_=gain_vectors[part].unsqueeze(0))
+        all_ones = const.tile([P, P], BF16)
+        nc.vector.memset(all_ones[:], 1.0)
+
         ones = const.tile([P, 1], F32)
         nc.vector.memset(ones[:], 1.0)
         warm = const.tile([P, 1], F32)
         nc.scalar.sqrt(out=warm[:], in_=ones[:])
 
-        x_codes = const.tile([P, PASSES, UNIT], U32, align_bytes=64)
-        x_scales = const.tile([P, PASSES, UNIT], U8, align_bytes=64)
-        gains = [const.tile([P, HIDDEN], BF16, name="gain%d" % part) for part in range(NORMED_PARTS)]
+        def spread_gain(part):
+            for i in range(CHUNKS_PER_PART):
+                columns = slice(i * CHUNK, (i + 1) * CHUNK)
+                bank = bank_pool.tile([P, 2, UNIT], F32)
+                row = bank[:].rearrange("p u r -> p (u r)")
+                nc.tensor.matmul(out=row, lhsT=all_ones[:], rhs=gain_rows[part][:, columns], start=True, stop=True)
+                if i % 2 == 0:
+                    nc.scalar.copy(out=gains[part][:, columns], in_=row)
+                else:
+                    nc.vector.tensor_copy(out=gains[part][:, columns], in_=row)
 
         def load_unit(rows):
             raw = raw_pool.tile([P, ROWS_PER_PARTITION, HIDDEN], BF16)
@@ -84,11 +102,7 @@ def tile_internattention_pa_kernel(tc, x, w_qkv, q_norm_w, k_norm_w, out_0, out_
 
         def load_chunk(c):
             first = c * CHUNK
-            raws = [load_unit(w_qkv[first + h * UNIT : first + (h + 1) * UNIT, :]) for h in range(UNITS_PER_CHUNK)]
-            part = c // CHUNKS_PER_PART
-            if part < NORMED_PARTS and c % CHUNKS_PER_PART == 1:
-                nc.sync.dma_start(out=gains[part][:], in_=gain_rows[part].partition_broadcast(P))
-            return raws
+            return [load_unit(w_qkv[first + h * UNIT : first + (h + 1) * UNIT, :]) for h in range(UNITS_PER_CHUNK)]
 
         def regroup_unit(raw, vector_helps):
             grouped = grouped_pool.tile([P, PASSES, UNIT * PACK], BF16, align_bytes=64)
@@ -173,7 +187,9 @@ def tile_internattention_pa_kernel(tc, x, w_qkv, q_norm_w, k_norm_w, out_0, out_
         for c in range(CHUNKS_AHEAD):
             raws.extend(load_chunk(c))
 
+        spread_gain(0)
         quantise_unit(regroup_unit(x_raw, True), x_codes, x_scales, 0)
+        spread_gain(1)
 
         regrouped = {}
         operands = {}
@@ -212,7 +228,7 @@ def tile_internattention_pa_kernel(tc, x, w_qkv, q_norm_w, k_norm_w, out_0, out_
                     divide_and_store(t, part - 1, rms[part - 1], normed[part - 1])
 
             if s < UNITS:
-                regrouped[s] = regroup_unit(raws[s], s % 2 == 1)
+                regrouped[s] = regroup_unit(raws[s], s % 2 == 1 or s >= NORMED_PARTS * CHUNKS_PER_PART * UNITS_PER_CHUNK)
 
             job = s - MULTIPLY_LAG
             if 0 <= job < UNITS:

@@ -7,6 +7,7 @@ F32 = mybir.dt.float32
 BF16 = mybir.dt.bfloat16
 U32 = mybir.dt.uint32
 U8 = mybir.dt.uint8
+I32 = mybir.dt.int32
 FP8X4 = mybir.dt.float8_e4m3fn_x4
 ALU = mybir.AluOpType
 ACT = mybir.ActivationFunctionType
@@ -74,7 +75,7 @@ def tile_internattention_pa_kernel(tc, x, w_qkv, q_norm_w, k_norm_w, out_0, out_
         gain_rows = [const.tile([P, HIDDEN], BF16, name="gain_row%d" % part) for part in range(NORMED_PARTS)]
         gains = [const.tile([P, HIDDEN], BF16, name="gain%d" % part) for part in range(NORMED_PARTS)]
         for part in range(NORMED_PARTS):
-            nc.vector.memset(gain_rows[part][:], 0.0)
+            nc.vector.memset(gain_rows[part][:].bitcast(I32), 0)
             nc.scalar.dma_start(out=gain_rows[part][0:1, :], in_=gain_vectors[part].unsqueeze(0))
         all_ones = const.tile([P, P], BF16)
         nc.vector.memset(all_ones[:], 1.0)
@@ -187,9 +188,7 @@ def tile_internattention_pa_kernel(tc, x, w_qkv, q_norm_w, k_norm_w, out_0, out_
         for c in range(CHUNKS_AHEAD):
             raws.extend(load_chunk(c))
 
-        spread_gain(0)
         quantise_unit(regroup_unit(x_raw, True), x_codes, x_scales, 0)
-        spread_gain(1)
 
         regrouped = {}
         operands = {}
@@ -230,6 +229,8 @@ def tile_internattention_pa_kernel(tc, x, w_qkv, q_norm_w, k_norm_w, out_0, out_
             if s < UNITS:
                 regrouped[s] = regroup_unit(raws[s], s % 2 == 1 or s >= NORMED_PARTS * CHUNKS_PER_PART * UNITS_PER_CHUNK)
 
+            if 1 <= s <= NORMED_PARTS:
+                spread_gain(s - 1)
             job = s - MULTIPLY_LAG
             if 0 <= job < UNITS:
                 accs[job] = multiply(job % TOKEN_TILES, *operands[job // TOKEN_TILES])

@@ -19,6 +19,7 @@ EPS = 1e-6
 PACK = 4
 K_PASS = P * PACK
 PASSES = HIDDEN // K_PASS
+HALVES = 2
 WORDS_PER_PASS = K_PASS // 2
 ROWS_PER_PARTITION = 2
 UNIT = P * ROWS_PER_PARTITION
@@ -30,10 +31,17 @@ PARTS = 3
 NORMED_PARTS = 2
 CHUNKS = PARTS * CHUNKS_PER_PART
 UNITS = CHUNKS * UNITS_PER_CHUNK
+JOBS = CHUNKS * TOKEN_TILES
 CHUNKS_AHEAD = 3
 QUANTISE_LAG = 1
 MULTIPLY_LAG = 3
 TAKE_LAG = 4
+GROUPED_BUFS = 4
+CODES_BUFS = 3
+OUT_BUFS = 4
+PSUM_BANKS = 8
+ACC_BANKS = TOKEN_TILES
+TRANSPOSE_BANKS = PSUM_BANKS - ACC_BANKS
 
 FLOPS = 2 * TOKENS * HIDDEN * PARTS * HIDDEN
 
@@ -58,14 +66,14 @@ def tile_internattention_pa_kernel(tc, x, w_qkv, q_norm_w, k_norm_w, out_0, out_
     with ExitStack() as ctx:
         const = ctx.enter_context(tc.tile_pool(name="const", bufs=1))
         raw_pool = ctx.enter_context(tc.tile_pool(name="raw", bufs=UNITS_PER_CHUNK * (CHUNKS_AHEAD + 1)))
-        grouped_pool = ctx.enter_context(tc.tile_pool(name="grouped", bufs=4))
-        codes_pool = ctx.enter_context(tc.tile_pool(name="codes", bufs=3))
+        grouped_pool = ctx.enter_context(tc.tile_pool(name="grouped", bufs=GROUPED_BUFS))
+        codes_pool = ctx.enter_context(tc.tile_pool(name="codes", bufs=CODES_BUFS))
         normed_pool = ctx.enter_context(tc.tile_pool(name="normed", bufs=NORMED_PARTS * TOKEN_TILES))
-        plain_pool = ctx.enter_context(tc.tile_pool(name="plain", bufs=4))
-        squares_pool = ctx.enter_context(tc.tile_pool(name="squares", bufs=4))
+        plain_pool = ctx.enter_context(tc.tile_pool(name="plain", bufs=OUT_BUFS))
+        squares_pool = ctx.enter_context(tc.tile_pool(name="squares", bufs=OUT_BUFS))
         stats_pool = ctx.enter_context(tc.tile_pool(name="stats", bufs=NORMED_PARTS))
-        bank_pool = ctx.enter_context(tc.psum_pool(name="bank", bufs=6))
-        acc_pool = ctx.enter_context(tc.psum_pool(name="acc", bufs=TOKEN_TILES))
+        bank_pool = ctx.enter_context(tc.psum_pool(name="bank", bufs=TRANSPOSE_BANKS))
+        acc_pool = ctx.enter_context(tc.psum_pool(name="acc", bufs=ACC_BANKS))
 
         identity = const.tile([P, P], F32)
         make_identity(nc, identity[:])
@@ -88,7 +96,7 @@ def tile_internattention_pa_kernel(tc, x, w_qkv, q_norm_w, k_norm_w, out_0, out_
         def spread_gain(part):
             for i in range(CHUNKS_PER_PART):
                 columns = slice(i * CHUNK, (i + 1) * CHUNK)
-                bank = bank_pool.tile([P, 2, UNIT], F32)
+                bank = bank_pool.tile([P, HALVES, UNIT], F32)
                 row = bank[:].rearrange("p u r -> p (u r)")
                 nc.tensor.matmul(out=row, lhsT=all_ones[:], rhs=gain_rows[part][:, columns], start=True, stop=True)
                 if i % 2 == 0:
@@ -108,8 +116,8 @@ def tile_internattention_pa_kernel(tc, x, w_qkv, q_norm_w, k_norm_w, out_0, out_
         def regroup_unit(raw, vector_helps):
             grouped = grouped_pool.tile([P, PASSES, UNIT * PACK], BF16, align_bytes=64)
             for g in range(PASSES):
-                bank = bank_pool.tile([P, 2, UNIT], F32)
-                for u in range(2):
+                bank = bank_pool.tile([P, HALVES, UNIT], F32)
+                for u in range(HALVES):
                     first_word = g * WORDS_PER_PASS + u * P
                     for j in range(ROWS_PER_PARTITION):
                         nc.tensor.transpose(
@@ -117,7 +125,7 @@ def tile_internattention_pa_kernel(tc, x, w_qkv, q_norm_w, k_norm_w, out_0, out_
                             raw[:, j, :].bitcast(F32)[:, first_word : first_word + P],
                             identity[:],
                         )
-                pairs = grouped[:, g, :].bitcast(F32).rearrange("p (r u) -> p r u", u=2)
+                pairs = grouped[:, g, :].bitcast(F32).rearrange("p (r u) -> p r u", u=HALVES)
                 if vector_helps and g == PASSES - 1:
                     nc.vector.tensor_copy(out=pairs, in_=bank[:].rearrange("p u r -> p r u"))
                 else:
@@ -181,7 +189,6 @@ def tile_internattention_pa_kernel(tc, x, w_qkv, q_norm_w, k_norm_w, out_0, out_
             nc.vector.tensor_scalar_mul(out=normed[t][:], in0=normed[t][:], scalar1=inverse[:])
             nc.sync.dma_start(out=outs[part][:, t, :], in_=normed[t][:])
 
-        ctx.enter_context(tc.manual_schedule())
 
         x_raw = load_unit(x_rows)
         raws = []
@@ -196,7 +203,7 @@ def tile_internattention_pa_kernel(tc, x, w_qkv, q_norm_w, k_norm_w, out_0, out_
         sumsq = {}
         normed = {}
         rms = {}
-        for s in range(UNITS + TAKE_LAG):
+        for s in range(JOBS + TAKE_LAG):
             if s % UNITS_PER_CHUNK == 0 and s // UNITS_PER_CHUNK + CHUNKS_AHEAD < CHUNKS:
                 raws.extend(load_chunk(s // UNITS_PER_CHUNK + CHUNKS_AHEAD))
 
@@ -210,7 +217,7 @@ def tile_internattention_pa_kernel(tc, x, w_qkv, q_norm_w, k_norm_w, out_0, out_
                 quantise_unit(regrouped[unit], *operands[c], unit % UNITS_PER_CHUNK)
 
             job = s - TAKE_LAG
-            if 0 <= job < UNITS:
+            if 0 <= job < JOBS:
                 t = job % TOKEN_TILES
                 part = job // TOKEN_TILES // CHUNKS_PER_PART
                 i = job // TOKEN_TILES % CHUNKS_PER_PART
@@ -227,12 +234,13 @@ def tile_internattention_pa_kernel(tc, x, w_qkv, q_norm_w, k_norm_w, out_0, out_
                     divide_and_store(t, part - 1, rms[part - 1], normed[part - 1])
 
             if s < UNITS:
-                regrouped[s] = regroup_unit(raws[s], s % 2 == 1 or s >= NORMED_PARTS * CHUNKS_PER_PART * UNITS_PER_CHUNK)
+                is_plain = s >= NORMED_PARTS * CHUNKS_PER_PART * UNITS_PER_CHUNK
+                regrouped[s] = regroup_unit(raws[s], s % 2 == 1 or is_plain)
 
             if 1 <= s <= NORMED_PARTS:
                 spread_gain(s - 1)
             job = s - MULTIPLY_LAG
-            if 0 <= job < UNITS:
+            if 0 <= job < JOBS:
                 accs[job] = multiply(job % TOKEN_TILES, *operands[job // TOKEN_TILES])
 
             job = s - TAKE_LAG

from contextlib import ExitStack

import concourse.mybir as mybir
from concourse.masks import make_identity

F32 = mybir.dt.float32
BF16 = mybir.dt.bfloat16
U32 = mybir.dt.uint32
U8 = mybir.dt.uint8
I32 = mybir.dt.int32
FP8X4 = mybir.dt.float8_e4m3fn_x4
ALU = mybir.AluOpType
ACT = mybir.ActivationFunctionType

P = 128
HIDDEN = 2048
TOKENS = 256
EPS = 1e-6
PACK = 4
K_PASS = P * PACK
PASSES = HIDDEN // K_PASS
HALVES = 2
WORDS_PER_PASS = K_PASS // 2
ROWS_PER_PARTITION = 2
UNIT = P * ROWS_PER_PARTITION
TOKEN_TILES = TOKENS // P
CHUNK = 512
UNITS_PER_CHUNK = CHUNK // UNIT
CHUNKS_PER_PART = HIDDEN // CHUNK
PARTS = 3
NORMED_PARTS = 2
CHUNKS = PARTS * CHUNKS_PER_PART
UNITS = CHUNKS * UNITS_PER_CHUNK
JOBS = CHUNKS * TOKEN_TILES
CHUNKS_AHEAD = 3
QUANTISE_LAG = 1
MULTIPLY_LAG = 3
TAKE_LAG = 4
GROUPED_BUFS = 4
CODES_BUFS = 3
OUT_BUFS = 4
PSUM_BANKS = 8
ACC_BANKS = TOKEN_TILES
TRANSPOSE_BANKS = PSUM_BANKS - ACC_BANKS

FLOPS = 2 * TOKENS * HIDDEN * PARTS * HIDDEN


def as_multiplied(columns):
    return columns.rearrange("m (h j p) -> m h p j", h=UNITS_PER_CHUNK, j=ROWS_PER_PARTITION)


def as_stored(columns):
    return columns.rearrange("m (h p j) -> m h p j", h=UNITS_PER_CHUNK, j=ROWS_PER_PARTITION)


def tile_internattention_pa_kernel(tc, x, w_qkv, q_norm_w, k_norm_w, out_0, out_1, out_2):
    nc = tc.nc
    x_rows = x.flatten_outer_dims()
    outs = [
        out.flatten_outer_dims().rearrange("(p t) n -> p t n", t=TOKEN_TILES)
        for out in (out_0, out_1, out_2)
    ]
    gain_vectors = [q_norm_w, k_norm_w]

    with ExitStack() as ctx:
        const = ctx.enter_context(tc.tile_pool(name="const", bufs=1))
        raw_pool = ctx.enter_context(tc.tile_pool(name="raw", bufs=UNITS_PER_CHUNK * (CHUNKS_AHEAD + 1)))
        grouped_pool = ctx.enter_context(tc.tile_pool(name="grouped", bufs=GROUPED_BUFS))
        codes_pool = ctx.enter_context(tc.tile_pool(name="codes", bufs=CODES_BUFS))
        normed_pool = ctx.enter_context(tc.tile_pool(name="normed", bufs=NORMED_PARTS * TOKEN_TILES))
        plain_pool = ctx.enter_context(tc.tile_pool(name="plain", bufs=OUT_BUFS))
        squares_pool = ctx.enter_context(tc.tile_pool(name="squares", bufs=OUT_BUFS))
        stats_pool = ctx.enter_context(tc.tile_pool(name="stats", bufs=NORMED_PARTS))
        bank_pool = ctx.enter_context(tc.psum_pool(name="bank", bufs=TRANSPOSE_BANKS))
        acc_pool = ctx.enter_context(tc.psum_pool(name="acc", bufs=ACC_BANKS))

        identity = const.tile([P, P], F32)
        make_identity(nc, identity[:])
        x_codes = const.tile([P, PASSES, UNIT], U32, align_bytes=64)
        x_scales = const.tile([P, PASSES, UNIT], U8, align_bytes=64)

        gain_rows = [const.tile([P, HIDDEN], BF16, name="gain_row%d" % part) for part in range(NORMED_PARTS)]
        gains = [const.tile([P, HIDDEN], BF16, name="gain%d" % part) for part in range(NORMED_PARTS)]
        for part in range(NORMED_PARTS):
            nc.vector.memset(gain_rows[part][:].bitcast(I32), 0)
            nc.scalar.dma_start(out=gain_rows[part][0:1, :], in_=gain_vectors[part].unsqueeze(0))
        all_ones = const.tile([P, P], BF16)
        nc.vector.memset(all_ones[:], 1.0)

        ones = const.tile([P, 1], F32)
        nc.vector.memset(ones[:], 1.0)
        warm = const.tile([P, 1], F32)
        nc.scalar.sqrt(out=warm[:], in_=ones[:])

        def spread_gain(part):
            for i in range(CHUNKS_PER_PART):
                columns = slice(i * CHUNK, (i + 1) * CHUNK)
                bank = bank_pool.tile([P, HALVES, UNIT], F32)
                row = bank[:].rearrange("p u r -> p (u r)")
                nc.tensor.matmul(out=row, lhsT=all_ones[:], rhs=gain_rows[part][:, columns], start=True, stop=True)
                if i % 2 == 0:
                    nc.scalar.copy(out=gains[part][:, columns], in_=row)
                else:
                    nc.vector.tensor_copy(out=gains[part][:, columns], in_=row)

        def load_unit(rows):
            raw = raw_pool.tile([P, ROWS_PER_PARTITION, HIDDEN], BF16)
            nc.sync.dma_start(out=raw[:], in_=rows.rearrange("(p j) k -> p j k", j=ROWS_PER_PARTITION))
            return raw

        def load_chunk(c):
            first = c * CHUNK
            return [load_unit(w_qkv[first + h * UNIT : first + (h + 1) * UNIT, :]) for h in range(UNITS_PER_CHUNK)]

        def regroup_unit(raw, vector_helps):
            grouped = grouped_pool.tile([P, PASSES, UNIT * PACK], BF16, align_bytes=64)
            for g in range(PASSES):
                bank = bank_pool.tile([P, HALVES, UNIT], F32)
                for u in range(HALVES):
                    first_word = g * WORDS_PER_PASS + u * P
                    for j in range(ROWS_PER_PARTITION):
                        nc.tensor.transpose(
                            bank[:, u, j * P : (j + 1) * P],
                            raw[:, j, :].bitcast(F32)[:, first_word : first_word + P],
                            identity[:],
                        )
                pairs = grouped[:, g, :].bitcast(F32).rearrange("p (r u) -> p r u", u=HALVES)
                if vector_helps and g == PASSES - 1:
                    nc.vector.tensor_copy(out=pairs, in_=bank[:].rearrange("p u r -> p r u"))
                else:
                    nc.scalar.copy(out=pairs, in_=bank[:].rearrange("p u r -> p r u"))
            return grouped

        def quantise_unit(grouped, codes, scales, h):
            columns = slice(h * UNIT, (h + 1) * UNIT)
            for g in range(PASSES):
                nc.vector.quantize_mx(
                    out=codes[:, g, columns].bitcast(FP8X4),
                    scales=scales[:, g, columns],
                    in_=grouped[:, g, :],
                )

        def multiply(t, codes, scales):
            acc = acc_pool.tile([P, CHUNK], F32)
            for g in range(PASSES):
                nc.tensor.matmul_mx(
                    out=acc[:],
                    lhsT=x_codes[:, g, t * P : (t + 1) * P].bitcast(FP8X4),
                    lhsT_scale=x_scales[:, g, t * P : (t + 1) * P],
                    rhs=codes[:, g, :].bitcast(FP8X4),
                    rhs_scale=scales[:, g, :],
                    start=(g == 0),
                    stop=(g == PASSES - 1),
                )
            return acc

        def take_normed(acc, t, part, i, sumsq, normed):
            columns = slice(i * CHUNK, (i + 1) * CHUNK)
            squares = squares_pool.tile([P, CHUNK], BF16)
            nc.scalar.activation(out=squares[:], in_=acc[:], func=ACT.Square, accum_out=sumsq[:, t, i : i + 1])
            nc.vector.tensor_tensor(
                out=as_stored(normed[t][:, columns]),
                in0=as_multiplied(acc[:]),
                in1=as_stored(gains[part][:, columns]),
                op=ALU.mult,
            )

        def take_plain(acc, t, i):
            columns = slice(i * CHUNK, (i + 1) * CHUNK)
            plain = plain_pool.tile([P, CHUNK], F32)
            nc.scalar.copy(out=as_stored(plain[:]), in_=as_multiplied(acc[:]))
            nc.sync.dma_start(out=outs[PARTS - 1][:, t, columns], in_=plain[:])

        def root_mean_square(sumsq):
            total = stats_pool.tile([P, TOKEN_TILES], F32)
            nc.vector.tensor_reduce(out=total[:], in_=sumsq[:], axis=mybir.AxisListType.X, op=ALU.add)
            mean = stats_pool.tile([P, TOKEN_TILES], F32)
            nc.vector.tensor_scalar(
                out=mean[:], in0=total[:], scalar1=1.0 / HIDDEN, scalar2=EPS, op0=ALU.mult, op1=ALU.add
            )
            rms = stats_pool.tile([P, TOKEN_TILES], F32)
            nc.scalar.sqrt(out=rms[:], in_=mean[:])
            return rms

        def divide_and_store(t, part, rms, normed):
            inverse = stats_pool.tile([P, 1], F32)
            nc.vector.reciprocal(out=inverse[:], in_=rms[:, t : t + 1])
            nc.vector.tensor_scalar_mul(out=normed[t][:], in0=normed[t][:], scalar1=inverse[:])
            nc.sync.dma_start(out=outs[part][:, t, :], in_=normed[t][:])


        x_raw = load_unit(x_rows)
        raws = []
        for c in range(CHUNKS_AHEAD):
            raws.extend(load_chunk(c))

        quantise_unit(regroup_unit(x_raw, True), x_codes, x_scales, 0)

        regrouped = {}
        operands = {}
        accs = {}
        sumsq = {}
        normed = {}
        rms = {}
        for s in range(JOBS + TAKE_LAG):
            if s % UNITS_PER_CHUNK == 0 and s // UNITS_PER_CHUNK + CHUNKS_AHEAD < CHUNKS:
                raws.extend(load_chunk(s // UNITS_PER_CHUNK + CHUNKS_AHEAD))

            unit = s - QUANTISE_LAG
            if 0 <= unit < UNITS:
                c = unit // UNITS_PER_CHUNK
                if unit % UNITS_PER_CHUNK == 0:
                    codes = codes_pool.tile([P, PASSES, CHUNK], U32, align_bytes=64)
                    scales = codes_pool.tile([P, PASSES, CHUNK], U8, align_bytes=64)
                    operands[c] = (codes, scales)
                quantise_unit(regrouped[unit], *operands[c], unit % UNITS_PER_CHUNK)

            job = s - TAKE_LAG
            if 0 <= job < JOBS:
                t = job % TOKEN_TILES
                part = job // TOKEN_TILES // CHUNKS_PER_PART
                i = job // TOKEN_TILES % CHUNKS_PER_PART
                if part < NORMED_PARTS:
                    if i == 0 and t == 0:
                        sumsq[part] = stats_pool.tile([P, TOKEN_TILES, CHUNKS_PER_PART], F32, name="sumsq")
                        normed[part] = [
                            normed_pool.tile([P, HIDDEN], F32, name="normed") for each in range(TOKEN_TILES)
                        ]
                    take_normed(accs[job], t, part, i, sumsq[part], normed[part])
                else:
                    take_plain(accs[job], t, i)
                if i == 0 and part > 0:
                    divide_and_store(t, part - 1, rms[part - 1], normed[part - 1])

            if s < UNITS:
                is_plain = s >= NORMED_PARTS * CHUNKS_PER_PART * UNITS_PER_CHUNK
                regrouped[s] = regroup_unit(raws[s], s % 2 == 1 or is_plain)

            if 1 <= s <= NORMED_PARTS:
                spread_gain(s - 1)
            job = s - MULTIPLY_LAG
            if 0 <= job < JOBS:
                accs[job] = multiply(job % TOKEN_TILES, *operands[job // TOKEN_TILES])

            job = s - TAKE_LAG
            if job >= 0 and job % (TOKEN_TILES * CHUNKS_PER_PART) == TOKEN_TILES * CHUNKS_PER_PART - 1:
                part = job // TOKEN_TILES // CHUNKS_PER_PART
                if part < NORMED_PARTS:
                    rms[part] = root_mean_square(sumsq[part])
